import numpy as np
import ml_dtypes


def mxq(x, axis, fmt="e4m3"):
    dtype, down = {"e4m3": (ml_dtypes.float8_e4m3fn, 7), "e5m2": (ml_dtypes.float8_e5m2, 14)}[fmt]
    v = np.moveaxis(np.asarray(x, np.float32).astype(ml_dtypes.bfloat16).astype(np.float64), axis, -1)
    blocks = v.reshape(v.shape[:-1] + (-1, 32))
    amax = np.abs(blocks).max(-1, keepdims=True)
    byte = np.maximum(np.where(amax > 0, np.frexp(amax)[1] - 1 + 127, 0) - down, 1)
    scale = np.exp2(byte - 127.0)
    codes = (blocks / scale).astype(np.float32).astype(dtype).astype(np.float64)
    return np.moveaxis((codes * scale).reshape(v.shape), -1, axis)


WIDE = False


def mx_kscale(k):
    if not WIDE:
        return np.ones(k)
    levels = np.array([20, -20, 10, -10, 0])
    a = np.random.permutation(np.resize(levels, k // 512 * 4)).reshape(k // 512, 4)
    idx = np.arange(k)
    return np.exp2(a[idx // 512, idx % 128 // 32])


BF16 = ml_dtypes.bfloat16


def bf(x):
    return np.asarray(x, np.float32).astype(BF16)


def f64(x):
    return np.asarray(x).astype(np.float64)


B, H0, C0, C1, C2, NA, NO = 6, 32, 512, 512, 1024, 4, 128
H1, H2 = H0 // 2, H0 // 4
O = NA * NO
P0 = H0 * H0
R0 = NA * P0
R = NA * (H0 * H0 + H1 * H1 + H2 * H2)


def sigmoid(v):
    return 1.0 / (1.0 + np.exp(-v))


def _draw_level(c, h):
    f = bf(np.random.standard_normal((B, c, h, h)))
    w = bf(np.random.standard_normal((O, c)) / np.sqrt(c))
    b = bf(np.random.standard_normal(O) * 0.5)
    return f, w, b


def setup_inputs():
    u = mx_kscale(O)
    f0, w00, b0 = _draw_level(C0, H0)
    f1, w1, b1 = _draw_level(C1, H1)
    f2, w2, b2 = _draw_level(C2, H2)
    anchors = bf(1.0 + 4.0 * np.random.random((3, NA, 2)))
    fac = np.ones((R, NO))
    fac[:R0] = np.repeat(u.reshape(NA, NO), P0, axis=0)
    g = bf(np.random.standard_normal((B, R, NO)) * np.exp2(np.random.randint(-12, 1, (B, R, 1))) * 4.0 * fac[None])
    wb = f64(w00).reshape(NA, NO, C0)[:, :4, :].reshape(NA * 4, C0)
    bb = f64(b0).reshape(NA, NO)[:, :4].reshape(NA * 4)
    z = wb @ f64(f0).reshape(B, C0, P0) + bb[None, :, None]
    z0 = z.reshape(B, NA, 4, P0).transpose(0, 1, 3, 2).reshape(B, R0, 4)
    w0 = bf(f64(w00) / u[:, None])
    return {"f0": f0, "f1": f1, "f2": f2, "w0": w0, "b0": b0, "w1": w1, "b1": b1, "w2": w2, "b2": b2,
            "anchors": anchors, "z0": np.asarray(z0, np.float32), "grad_out": g}


def reference(f0, f1, f2, w0, b0, w1, b1, w2, b2, anchors, z0, grad_out):
    g = f64(grad_out)[:, :R0, :]
    sg = sigmoid(f64(z0))
    a0 = np.repeat(f64(anchors)[0], P0, axis=0)
    dxy = g[..., 0:2] * (2.0 * sg[..., 0:2] * (1.0 - sg[..., 0:2]))
    dwh = g[..., 2:4] * (8.0 * np.square(sg[..., 2:4]) * (1.0 - sg[..., 2:4])) * a0[None]
    dy = np.concatenate([dxy, dwh, g[..., 4:]], axis=-1)
    dy = dy.reshape(B, NA, P0, NO).transpose(0, 1, 3, 2).reshape(B, O, P0)
    df = mxq(f64(w0), 0, "e4m3").T @ mxq(dy, 1, "e5m2")
    return df.reshape(B, C0, H0, H0)

@@ -1,0 +1,188 @@
+from contextlib import ExitStack
+
+import concourse.masks as masks
+import concourse.mybir as mybir
+
+F32 = mybir.dt.float32
+BF16 = mybir.dt.bfloat16
+U32 = mybir.dt.uint32
+U8 = mybir.dt.uint8
+E4M3_X4 = mybir.dt.float8_e4m3fn_x4
+E5M2_X4 = mybir.dt.float8_e5m2_x4
+ALU = mybir.AluOpType
+ACT = mybir.ActivationFunctionType
+
+P = 128
+IMAGES = 6
+ANCHORS = 4
+FIELDS = 128
+BOX = 4
+POSITIONS = 1024
+CHANNELS = 512
+LEVEL0_ROWS = ANCHORS * POSITIONS
+
+STRIPS = P // ANCHORS
+STRIP = POSITIONS // STRIPS
+N_TILE = 512
+HALF_T = N_TILE // STRIPS
+HALVES = STRIP // HALF_T
+T_PER_BANK = 8
+C_TILES = CHANNELS // P
+C_TILES_PER_STORE = 2
+
+FLOPS = 2 * ANCHORS * FIELDS * CHANNELS * IMAGES * POSITIONS
+BYTES = (
+    2 * IMAGES * LEVEL0_ROWS * FIELDS
+    + 4 * IMAGES * LEVEL0_ROWS * BOX
+    + 2 * ANCHORS * FIELDS * CHANNELS
+    + 2 * ANCHORS * 2
+    + 4 * IMAGES * CHANNELS * POSITIONS
+)
+
+
+def tile_head_t_v_kernel(
+    tc, f0, f1, f2, w0, b0, w1, b1, w2, b2, anchors, z0, grad_out, out
+):
+    nc = tc.nc
+    with ExitStack() as ctx:
+        ctx.enter_context(tc.manual_schedule())
+        const = ctx.enter_context(tc.tile_pool(name="const", bufs=1))
+        grads = ctx.enter_context(tc.tile_pool(name="grads", bufs=IMAGES))
+        operands = ctx.enter_context(tc.tile_pool(name="operands", bufs=3))
+        results = ctx.enter_context(tc.tile_pool(name="results", bufs=4))
+        flipped = ctx.enter_context(tc.psum_pool(name="flipped", bufs=4))
+        sums = ctx.enter_context(tc.psum_pool(name="sums", bufs=4))
+
+        z_sb = const.tile([P, IMAGES * STRIP * BOX], F32)
+        nc.sync.dma_start(
+            out=z_sb[:].rearrange("p (n f) -> p n f", n=IMAGES),
+            in_=z0.rearrange("n (p t) j -> p n (t j)", p=P),
+        )
+        anchors_sb = const.tile([P, ANCHORS * 2], BF16)
+        nc.sync.dma_start(
+            out=anchors_sb[:], in_=anchors[0].rearrange("a c -> (a c)").partition_broadcast(P)
+        )
+        w_sb = const.tile([P, ANCHORS * CHANNELS], BF16)
+        dy_tiles = []
+        for n in range(IMAGES):
+            dy_sb = grads.tile([P, STRIP * FIELDS], BF16)
+            nc.sync.dma_start(
+                out=dy_sb[:], in_=grad_out[n, 0:LEVEL0_ROWS, :].rearrange("(p t) j -> p (t j)", p=P)
+            )
+            dy_tiles.append(dy_sb)
+            if n == 0:
+                nc.sync.dma_start(
+                    out=w_sb[:].rearrange("p (a c) -> p a c", a=ANCHORS),
+                    in_=w0.rearrange("(a p) c -> p a c", a=ANCHORS),
+                )
+
+        identity = const.tile([P, P], BF16)
+        masks.make_identity(nc, identity[:])
+        anchors_together = const.tile([P, P], BF16)
+        nc.vector.tensor_copy(
+            out=anchors_together[:].rearrange("p (s a) -> p s a", a=ANCHORS),
+            in_=identity[:].rearrange("p (a s) -> p s a", a=ANCHORS),
+        )
+
+        minus_8_anchor = const.tile([P, 2], F32)
+        for a in range(ANCHORS):
+            rows = slice(a * STRIPS, (a + 1) * STRIPS)
+            nc.vector.tensor_scalar_mul(
+                out=minus_8_anchor[rows, :], in0=anchors_sb[rows, 2 * a : 2 * a + 2], scalar1=-8.0
+            )
+        sg = const.tile([P, IMAGES * STRIP * BOX], F32)
+        nc.scalar.activation(out=sg[:], in_=z_sb[:], func=ACT.Sigmoid)
+        minus_slope = const.tile([P, IMAGES * STRIP * BOX], F32)
+        nc.vector.scalar_tensor_tensor(
+            out=minus_slope[:], in0=sg[:], scalar=1.0, in1=sg[:], op0=ALU.subtract, op1=ALU.mult
+        )
+        factor = const.tile([P, BOX * IMAGES * STRIP], F32)
+        factor_planes = factor[:].rearrange("p (j r) -> p j r", j=BOX)
+        sg_planes = sg[:].rearrange("p (r j) -> p j r", j=BOX)
+        minus_slope_planes = minus_slope[:].rearrange("p (r j) -> p j r", j=BOX)
+        nc.vector.tensor_scalar_mul(
+            out=factor_planes[:, 0:2, :], in0=minus_slope_planes[:, 0:2, :], scalar1=-2.0
+        )
+        for c in range(2):
+            nc.vector.scalar_tensor_tensor(
+                out=factor_planes[:, 2 + c, :],
+                in0=minus_slope_planes[:, 2 + c, :],
+                scalar=minus_8_anchor[:, c : c + 1],
+                in1=sg_planes[:, 2 + c, :],
+                op0=ALU.mult,
+                op1=ALU.mult,
+            )
+
+        w_grouped = const.tile([P, C_TILES * P * ANCHORS], BF16, align_bytes=64)
+        nc.scalar.copy(
+            out=w_grouped[:].rearrange("p (ct m a) -> p ct m a", ct=C_TILES, a=ANCHORS),
+            in_=w_sb[:].rearrange("p (a m ct) -> p ct m a", a=ANCHORS, ct=C_TILES),
+        )
+        w_codes = const.tile([P, CHANNELS], U32, align_bytes=64)
+        w_scales = const.tile([P, CHANNELS], U8, align_bytes=64)
+
+        def prepare(n, half):
+            dy_sb = dy_tiles[n]
+            if half == 0:
+                box = dy_sb[:].rearrange("p (t j) -> p t j", j=FIELDS)[:, :, 0:BOX]
+                nc.vector.tensor_tensor(
+                    out=box,
+                    in0=box,
+                    in1=factor[:].rearrange("p (j n t) -> p n t j", j=BOX, n=IMAGES)[:, n],
+                    op=ALU.mult,
+                )
+            dy_grouped = operands.tile([P, N_TILE * ANCHORS], BF16, align_bytes=64)
+            for bank in range(HALF_T // T_PER_BANK):
+                dy_t = flipped.tile([P, T_PER_BANK * P], BF16)
+                for i in range(T_PER_BANK):
+                    t = half * HALF_T + bank * T_PER_BANK + i
+                    nc.tensor.transpose(
+                        dy_t[:, i * P : (i + 1) * P],
+                        dy_sb[:, t * FIELDS : (t + 1) * FIELDS],
+                        anchors_together[:],
+                    )
+                width = T_PER_BANK * P
+                nc.vector.tensor_copy(
+                    out=dy_grouped[:, bank * width : (bank + 1) * width], in_=dy_t[:]
+                )
+            dy_codes = operands.tile([P, N_TILE], U32, align_bytes=64)
+            dy_scales = operands.tile([P, N_TILE], U8, align_bytes=64)
+            nc.vector.quantize_mx(
+                out=dy_codes[:].bitcast(E5M2_X4), scales=dy_scales[:], in_=dy_grouped[:]
+            )
+            return dy_codes, dy_scales
+
+        def multiply(n, half, dy_codes, dy_scales, out_sb):
+            out_view = out_sb[:].rearrange("p (ct s t) -> p ct s t", ct=C_TILES, s=STRIPS)
+            for ct in range(C_TILES):
+                acc = sums.tile([P, N_TILE], F32)
+                nc.tensor.matmul_mx(
+                    out=acc[:],
+                    lhsT=w_codes[:, ct * P : (ct + 1) * P].bitcast(E4M3_X4),
+                    lhsT_scale=w_scales[:, ct * P : (ct + 1) * P],
+                    rhs=dy_codes[:].bitcast(E5M2_X4),
+                    rhs_scale=dy_scales[:],
+                    start=True,
+                    stop=True,
+                )
+                nc.scalar.copy(
+                    out=out_view[:, ct, :, half * HALF_T : (half + 1) * HALF_T],
+                    in_=acc[:].rearrange("p (t s) -> p s t", s=STRIPS),
+                )
+                if half == HALVES - 1 and (ct + 1) % C_TILES_PER_STORE == 0:
+                    cols = slice((ct + 1 - C_TILES_PER_STORE) * POSITIONS, (ct + 1) * POSITIONS)
+                    nc.sync.dma_start(
+                        out=out[n].rearrange("(m ct) u v -> m (ct u v)", ct=C_TILES)[:, cols],
+                        in_=out_sb[:, cols],
+                    )
+
+        units = [(n, half) for n in range(IMAGES) for half in range(HALVES)]
+        ready = prepare(0, 0)
+        nc.vector.quantize_mx(out=w_codes[:].bitcast(E4M3_X4), scales=w_scales[:], in_=w_grouped[:])
+        out_sb = None
+        for u, (n, half) in enumerate(units):
+            following = prepare(units[u + 1][0], units[u + 1][1]) if u + 1 < len(units) else None
+            if half == 0:
+                out_sb = results.tile([P, C_TILES * POSITIONS], F32)
+            multiply(n, half, ready[0], ready[1], out_sb)
+            ready = following

@@ -48,19 +48,20 @@ def tile_head_t_v_kernel(
         ctx.enter_context(tc.manual_schedule())
         const = ctx.enter_context(tc.tile_pool(name="const", bufs=1))
         grads = ctx.enter_context(tc.tile_pool(name="grads", bufs=IMAGES))
+        factors = ctx.enter_context(tc.tile_pool(name="factors", bufs=2))
         operands = ctx.enter_context(tc.tile_pool(name="operands", bufs=3))
         results = ctx.enter_context(tc.tile_pool(name="results", bufs=4))
         flipped = ctx.enter_context(tc.psum_pool(name="flipped", bufs=4))
         sums = ctx.enter_context(tc.psum_pool(name="sums", bufs=4))
 
+        anchors_sb = const.tile([P, ANCHORS * 2], BF16)
+        nc.sync.dma_start(
+            out=anchors_sb[:], in_=anchors[0].rearrange("a c -> (a c)").partition_broadcast(P)
+        )
         z_sb = const.tile([P, IMAGES * STRIP * BOX], F32)
         nc.sync.dma_start(
             out=z_sb[:].rearrange("p (n f) -> p n f", n=IMAGES),
             in_=z0.rearrange("n (p t) j -> p n (t j)", p=P),
-        )
-        anchors_sb = const.tile([P, ANCHORS * 2], BF16)
-        nc.sync.dma_start(
-            out=anchors_sb[:], in_=anchors[0].rearrange("a c -> (a c)").partition_broadcast(P)
         )
         w_sb = const.tile([P, ANCHORS * CHANNELS], BF16)
         dy_tiles = []
@@ -92,59 +93,66 @@ def tile_head_t_v_kernel(
             )
         sg = const.tile([P, IMAGES * STRIP * BOX], F32)
         nc.scalar.activation(out=sg[:], in_=z_sb[:], func=ACT.Sigmoid)
-        minus_slope = const.tile([P, IMAGES * STRIP * BOX], F32)
-        nc.vector.scalar_tensor_tensor(
-            out=minus_slope[:], in0=sg[:], scalar=1.0, in1=sg[:], op0=ALU.subtract, op1=ALU.mult
-        )
-        factor = const.tile([P, BOX * IMAGES * STRIP], F32)
-        factor_planes = factor[:].rearrange("p (j r) -> p j r", j=BOX)
-        sg_planes = sg[:].rearrange("p (r j) -> p j r", j=BOX)
-        minus_slope_planes = minus_slope[:].rearrange("p (r j) -> p j r", j=BOX)
-        nc.vector.tensor_scalar_mul(
-            out=factor_planes[:, 0:2, :], in0=minus_slope_planes[:, 0:2, :], scalar1=-2.0
-        )
-        for c in range(2):
+
+        def scale_box_fields(n):
+            sg_n = sg[:, n * STRIP * BOX : (n + 1) * STRIP * BOX]
+            minus_slope = factors.tile([P, STRIP * BOX], F32)
             nc.vector.scalar_tensor_tensor(
-                out=factor_planes[:, 2 + c, :],
-                in0=minus_slope_planes[:, 2 + c, :],
-                scalar=minus_8_anchor[:, c : c + 1],
-                in1=sg_planes[:, 2 + c, :],
-                op0=ALU.mult,
-                op1=ALU.mult,
+                out=minus_slope[:], in0=sg_n, scalar=1.0, in1=sg_n, op0=ALU.subtract, op1=ALU.mult
+            )
+            factor = factors.tile([P, BOX * STRIP], F32)
+            factor_planes = factor[:].rearrange("p (j t) -> p j t", j=BOX)
+            sg_planes = sg_n.rearrange("p (t j) -> p j t", j=BOX)
+            minus_slope_planes = minus_slope[:].rearrange("p (t j) -> p j t", j=BOX)
+            nc.vector.tensor_scalar_mul(
+                out=factor_planes[:, 0:2, :], in0=minus_slope_planes[:, 0:2, :], scalar1=-2.0
+            )
+            for c in range(2):
+                nc.vector.scalar_tensor_tensor(
+                    out=factor_planes[:, 2 + c, :],
+                    in0=minus_slope_planes[:, 2 + c, :],
+                    scalar=minus_8_anchor[:, c : c + 1],
+                    in1=sg_planes[:, 2 + c, :],
+                    op0=ALU.mult,
+                    op1=ALU.mult,
+                )
+            box = dy_tiles[n][:].rearrange("p (t j) -> p t j", j=FIELDS)[:, :, 0:BOX]
+            nc.vector.tensor_tensor(
+                out=box, in0=box, in1=factor[:].rearrange("p (j t) -> p t j", j=BOX), op=ALU.mult
             )
 
-        w_grouped = const.tile([P, C_TILES * P * ANCHORS], BF16, align_bytes=64)
-        nc.scalar.copy(
-            out=w_grouped[:].rearrange("p (ct m a) -> p ct m a", ct=C_TILES, a=ANCHORS),
-            in_=w_sb[:].rearrange("p (a m ct) -> p ct m a", a=ANCHORS, ct=C_TILES),
-        )
-        w_codes = const.tile([P, CHANNELS], U32, align_bytes=64)
-        w_scales = const.tile([P, CHANNELS], U8, align_bytes=64)
+        def quantise_weights():
+            w_grouped = const.tile([P, C_TILES * P * ANCHORS], BF16, align_bytes=64)
+            nc.vector.tensor_copy(
+                out=w_grouped[:].rearrange("p (ct m a) -> p ct m a", ct=C_TILES, a=ANCHORS),
+                in_=w_sb[:].rearrange("p (a m ct) -> p ct m a", a=ANCHORS, ct=C_TILES),
+            )
+            w_codes = const.tile([P, CHANNELS], U32, align_bytes=64)
+            w_scales = const.tile([P, CHANNELS], U8, align_bytes=64)
+            nc.vector.quantize_mx(
+                out=w_codes[:].bitcast(E4M3_X4), scales=w_scales[:], in_=w_grouped[:]
+            )
+            return w_codes, w_scales
 
-        def prepare(n, half):
-            dy_sb = dy_tiles[n]
-            if half == 0:
-                box = dy_sb[:].rearrange("p (t j) -> p t j", j=FIELDS)[:, :, 0:BOX]
-                nc.vector.tensor_tensor(
-                    out=box,
-                    in0=box,
-                    in1=factor[:].rearrange("p (j n t) -> p n t j", j=BOX, n=IMAGES)[:, n],
-                    op=ALU.mult,
-                )
+        def transpose(n, half):
             dy_grouped = operands.tile([P, N_TILE * ANCHORS], BF16, align_bytes=64)
+            width = T_PER_BANK * P
             for bank in range(HALF_T // T_PER_BANK):
-                dy_t = flipped.tile([P, T_PER_BANK * P], BF16)
+                dy_t = flipped.tile([P, width], BF16)
                 for i in range(T_PER_BANK):
                     t = half * HALF_T + bank * T_PER_BANK + i
                     nc.tensor.transpose(
                         dy_t[:, i * P : (i + 1) * P],
-                        dy_sb[:, t * FIELDS : (t + 1) * FIELDS],
+                        dy_tiles[n][:, t * FIELDS : (t + 1) * FIELDS],
                         anchors_together[:],
                     )
-                width = T_PER_BANK * P
-                nc.vector.tensor_copy(
-                    out=dy_grouped[:, bank * width : (bank + 1) * width], in_=dy_t[:]
+                nc.scalar.copy(
+                    out=dy_grouped[:, bank * width : (bank + 1) * width].bitcast(F32),
+                    in_=dy_t[:].bitcast(F32),
                 )
+            return dy_grouped
+
+        def quantise(dy_grouped):
             dy_codes = operands.tile([P, N_TILE], U32, align_bytes=64)
             dy_scales = operands.tile([P, N_TILE], U8, align_bytes=64)
             nc.vector.quantize_mx(
@@ -165,7 +173,8 @@ def tile_head_t_v_kernel(
                     start=True,
                     stop=True,
                 )
-                nc.scalar.copy(
+                copy_out = nc.scalar.copy if ct % 2 == 0 else nc.vector.tensor_copy
+                copy_out(
                     out=out_view[:, ct, :, half * HALF_T : (half + 1) * HALF_T],
                     in_=acc[:].rearrange("p (t s) -> p s t", s=STRIPS),
                 )
@@ -176,13 +185,23 @@ def tile_head_t_v_kernel(
                         in_=out_sb[:, cols],
                     )
 
+        scale_box_fields(0)
+        w_codes, w_scales = quantise_weights()
         units = [(n, half) for n in range(IMAGES) for half in range(HALVES)]
-        ready = prepare(0, 0)
-        nc.vector.quantize_mx(out=w_codes[:].bitcast(E4M3_X4), scales=w_scales[:], in_=w_grouped[:])
-        out_sb = None
-        for u, (n, half) in enumerate(units):
-            following = prepare(units[u + 1][0], units[u + 1][1]) if u + 1 < len(units) else None
-            if half == 0:
-                out_sb = results.tile([P, C_TILES * POSITIONS], F32)
-            multiply(n, half, ready[0], ready[1], out_sb)
-            ready = following
+        grouped_of = {}
+        codes_of = {}
+        out_of = {}
+        for step in range(len(units) + 2):
+            if step < len(units):
+                n, half = units[step]
+                grouped_of[step] = transpose(n, half)
+            if 1 <= step <= len(units):
+                codes_of[step - 1] = quantise(grouped_of[step - 1])
+            if step >= 2:
+                n, half = units[step - 2]
+                if half == 0:
+                    out_sb = results.tile([P, C_TILES * POSITIONS], F32)
+                    out_of[n] = out_sb
+                multiply(n, half, codes_of[step - 2][0], codes_of[step - 2][1], out_of[n])
+            if step < len(units) and units[step][1] == 0 and units[step][0] + 1 < IMAGES:
+                scale_box_fields(units[step][0] + 1)

@@ -28,7 +28,7 @@ HALF_T = N_TILE // STRIPS
 HALVES = STRIP // HALF_T
 T_PER_BANK = 8
 C_TILES = CHANNELS // P
-C_TILES_PER_STORE = 2
+C_TILES_PER_STEP = 2
 
 FLOPS = 2 * ANCHORS * FIELDS * CHANNELS * IMAGES * POSITIONS
 BYTES = (
@@ -49,7 +49,7 @@ def tile_head_t_v_kernel(
         const = ctx.enter_context(tc.tile_pool(name="const", bufs=1))
         grads = ctx.enter_context(tc.tile_pool(name="grads", bufs=IMAGES))
         factors = ctx.enter_context(tc.tile_pool(name="factors", bufs=2))
-        operands = ctx.enter_context(tc.tile_pool(name="operands", bufs=3))
+        operands = ctx.enter_context(tc.tile_pool(name="operands", bufs=6))
         results = ctx.enter_context(tc.tile_pool(name="results", bufs=4))
         flipped = ctx.enter_context(tc.psum_pool(name="flipped", bufs=4))
         sums = ctx.enter_context(tc.psum_pool(name="sums", bufs=4))
@@ -160,48 +160,49 @@ def tile_head_t_v_kernel(
             )
             return dy_codes, dy_scales
 
-        def multiply(n, half, dy_codes, dy_scales, out_sb):
+        def multiply(n, pair, operand_of_half, out_sb):
             out_view = out_sb[:].rearrange("p (ct s t) -> p ct s t", ct=C_TILES, s=STRIPS)
-            for ct in range(C_TILES):
-                acc = sums.tile([P, N_TILE], F32)
-                nc.tensor.matmul_mx(
-                    out=acc[:],
-                    lhsT=w_codes[:, ct * P : (ct + 1) * P].bitcast(E4M3_X4),
-                    lhsT_scale=w_scales[:, ct * P : (ct + 1) * P],
-                    rhs=dy_codes[:].bitcast(E5M2_X4),
-                    rhs_scale=dy_scales[:],
-                    start=True,
-                    stop=True,
-                )
-                copy_out = nc.scalar.copy if ct % 2 == 0 else nc.vector.tensor_copy
-                copy_out(
-                    out=out_view[:, ct, :, half * HALF_T : (half + 1) * HALF_T],
-                    in_=acc[:].rearrange("p (t s) -> p s t", s=STRIPS),
-                )
-                if half == HALVES - 1 and (ct + 1) % C_TILES_PER_STORE == 0:
-                    cols = slice((ct + 1 - C_TILES_PER_STORE) * POSITIONS, (ct + 1) * POSITIONS)
-                    nc.sync.dma_start(
-                        out=out[n].rearrange("(m ct) u v -> m (ct u v)", ct=C_TILES)[:, cols],
-                        in_=out_sb[:, cols],
+            for ct in range(pair * C_TILES_PER_STEP, (pair + 1) * C_TILES_PER_STEP):
+                for half in range(HALVES):
+                    dy_codes, dy_scales = operand_of_half[half]
+                    acc = sums.tile([P, N_TILE], F32)
+                    nc.tensor.matmul_mx(
+                        out=acc[:],
+                        lhsT=w_codes[:, ct * P : (ct + 1) * P].bitcast(E4M3_X4),
+                        lhsT_scale=w_scales[:, ct * P : (ct + 1) * P],
+                        rhs=dy_codes[:].bitcast(E5M2_X4),
+                        rhs_scale=dy_scales[:],
+                        start=True,
+                        stop=True,
                     )
+                    copy_out = nc.scalar.copy if half == 0 else nc.vector.tensor_copy
+                    copy_out(
+                        out=out_view[:, ct, :, half * HALF_T : (half + 1) * HALF_T],
+                        in_=acc[:].rearrange("p (t s) -> p s t", s=STRIPS),
+                    )
+                cols = slice(ct * POSITIONS, (ct + 1) * POSITIONS)
+                nc.sync.dma_start(
+                    out=out[n].rearrange("(m ct) u v -> m (ct u v)", ct=C_TILES)[:, cols],
+                    in_=out_sb[:, cols],
+                )
 
         scale_box_fields(0)
         w_codes, w_scales = quantise_weights()
-        units = [(n, half) for n in range(IMAGES) for half in range(HALVES)]
+        steps = IMAGES * HALVES
         grouped_of = {}
-        codes_of = {}
+        operand_of = {}
         out_of = {}
-        for step in range(len(units) + 2):
-            if step < len(units):
-                n, half = units[step]
+        for step in range(steps + 3):
+            if step < steps:
+                n, half = divmod(step, HALVES)
                 grouped_of[step] = transpose(n, half)
-            if 1 <= step <= len(units):
-                codes_of[step - 1] = quantise(grouped_of[step - 1])
-            if step >= 2:
-                n, half = units[step - 2]
-                if half == 0:
+            if 1 <= step <= steps:
+                operand_of[step - 1] = quantise(grouped_of[step - 1])
+            if step >= 3:
+                n, pair = divmod(step - 3, C_TILES // C_TILES_PER_STEP)
+                if pair == 0:
                     out_sb = results.tile([P, C_TILES * POSITIONS], F32)
                     out_of[n] = out_sb
-                multiply(n, half, codes_of[step - 2][0], codes_of[step - 2][1], out_of[n])
-            if step < len(units) and units[step][1] == 0 and units[step][0] + 1 < IMAGES:
-                scale_box_fields(units[step][0] + 1)
+                multiply(n, pair, [operand_of[n * HALVES + h] for h in range(HALVES)], out_of[n])
+            if step < steps and step % HALVES == 0 and step // HALVES + 1 < IMAGES:
+                scale_box_fields(step // HALVES + 1)

@@ -28,6 +28,7 @@ HALF_T = N_TILE // STRIPS
 HALVES = STRIP // HALF_T
 T_PER_BANK = 8
 C_TILES = CHANNELS // P
+SPREAD_N = 32
 C_TILES_PER_STEP = 2
 
 FLOPS = 2 * ANCHORS * FIELDS * CHANNELS * IMAGES * POSITIONS
@@ -54,15 +55,14 @@ def tile_head_t_v_kernel(
         flipped = ctx.enter_context(tc.psum_pool(name="flipped", bufs=4))
         sums = ctx.enter_context(tc.psum_pool(name="sums", bufs=4))
 
-        anchors_sb = const.tile([P, ANCHORS * 2], BF16)
-        nc.sync.dma_start(
-            out=anchors_sb[:], in_=anchors[0].rearrange("a c -> (a c)").partition_broadcast(P)
-        )
         z_sb = const.tile([P, IMAGES * STRIP * BOX], F32)
         nc.sync.dma_start(
             out=z_sb[:].rearrange("p (n f) -> p n f", n=IMAGES),
             in_=z0.rearrange("n (p t) j -> p n (t j)", p=P),
         )
+        anchor_rows = const.tile([P, SPREAD_N], BF16)
+        nc.vector.memset(anchor_rows[:], 0.0)
+        nc.sync.dma_start(out=anchor_rows[0:P:STRIPS, 0:2], in_=anchors[0])
         w_sb = const.tile([P, ANCHORS * CHANNELS], BF16)
         dy_tiles = []
         for n in range(IMAGES):
@@ -85,12 +85,21 @@ def tile_head_t_v_kernel(
             in_=identity[:].rearrange("p (a s) -> p s a", a=ANCHORS),
         )
 
-        minus_8_anchor = const.tile([P, 2], F32)
+        same_anchor = const.tile([P, P], BF16)
+        nc.vector.memset(same_anchor[:], 0.0)
         for a in range(ANCHORS):
-            rows = slice(a * STRIPS, (a + 1) * STRIPS)
-            nc.vector.tensor_scalar_mul(
-                out=minus_8_anchor[rows, :], in0=anchors_sb[rows, 2 * a : 2 * a + 2], scalar1=-8.0
-            )
+            block = slice(a * STRIPS, (a + 1) * STRIPS)
+            nc.vector.memset(same_anchor[block, block], 1.0)
+        own_anchor = sums.tile([P, N_TILE], F32, tag="acc")
+        nc.tensor.matmul(
+            out=own_anchor[:, 0:SPREAD_N],
+            lhsT=same_anchor[:],
+            rhs=anchor_rows[:],
+            start=True,
+            stop=True,
+        )
+        minus_8_anchor = const.tile([P, 2], F32)
+        nc.vector.tensor_scalar_mul(out=minus_8_anchor[:], in0=own_anchor[:, 0:2], scalar1=-8.0)
         sg = const.tile([P, IMAGES * STRIP * BOX], F32)
         nc.scalar.activation(out=sg[:], in_=z_sb[:], func=ACT.Sigmoid)
 
@@ -142,7 +151,7 @@ def tile_head_t_v_kernel(
                 for i in range(T_PER_BANK):
                     t = half * HALF_T + bank * T_PER_BANK + i
                     nc.tensor.transpose(
-                        dy_t[:, i * P : (i + 1) * P],
+                        dy_t[:].rearrange("p (s i a) -> p i s a", i=T_PER_BANK, a=ANCHORS)[:, i],
                         dy_tiles[n][:, t * FIELDS : (t + 1) * FIELDS],
                         anchors_together[:],
                     )
@@ -161,7 +170,9 @@ def tile_head_t_v_kernel(
             return dy_codes, dy_scales
 
         def multiply(n, pair, operand_of_half, out_sb):
-            out_view = out_sb[:].rearrange("p (ct s t) -> p ct s t", ct=C_TILES, s=STRIPS)
+            out_view = out_sb[:].rearrange(
+                "p (ct s h b i) -> p ct h b s i", ct=C_TILES, s=STRIPS, h=HALVES, i=T_PER_BANK
+            )
             for ct in range(pair * C_TILES_PER_STEP, (pair + 1) * C_TILES_PER_STEP):
                 for half in range(HALVES):
                     dy_codes, dy_scales = operand_of_half[half]
@@ -177,8 +188,8 @@ def tile_head_t_v_kernel(
                     )
                     copy_out = nc.scalar.copy if half == 0 else nc.vector.tensor_copy
                     copy_out(
-                        out=out_view[:, ct, :, half * HALF_T : (half + 1) * HALF_T],
-                        in_=acc[:].rearrange("p (t s) -> p s t", s=STRIPS),
+                        out=out_view[:, ct, half],
+                        in_=acc[:].rearrange("p (b s i) -> p b s i", s=STRIPS, i=T_PER_BANK),
                     )
                 cols = slice(ct * POSITIONS, (ct + 1) * POSITIONS)
                 nc.sync.dma_start(

@@ -29,6 +29,9 @@ HALVES = STRIP // HALF_T
 T_PER_BANK = 8
 C_TILES = CHANNELS // P
 SPREAD_N = 32
+EARLY = 2
+WARM_BEFORE_LOADS = 6
+WARM_AFTER_ANCHORS = 2
 C_TILES_PER_STEP = 2
 
 FLOPS = 2 * ANCHORS * FIELDS * CHANNELS * IMAGES * POSITIONS
@@ -48,34 +51,67 @@ def tile_head_t_v_kernel(
     with ExitStack() as ctx:
         ctx.enter_context(tc.manual_schedule())
         const = ctx.enter_context(tc.tile_pool(name="const", bufs=1))
-        grads = ctx.enter_context(tc.tile_pool(name="grads", bufs=IMAGES))
+        pieces = ctx.enter_context(tc.tile_pool(name="pieces", bufs=STRIP // T_PER_BANK))
+        grads = ctx.enter_context(tc.tile_pool(name="grads", bufs=IMAGES - 1))
         factors = ctx.enter_context(tc.tile_pool(name="factors", bufs=2))
         operands = ctx.enter_context(tc.tile_pool(name="operands", bufs=6))
         results = ctx.enter_context(tc.tile_pool(name="results", bufs=4))
         flipped = ctx.enter_context(tc.psum_pool(name="flipped", bufs=4))
         sums = ctx.enter_context(tc.psum_pool(name="sums", bufs=4))
 
-        z_sb = const.tile([P, IMAGES * STRIP * BOX], F32)
+        ones = const.tile([P, N_TILE], BF16)
+        nc.vector.memset(ones[:], 1.0)
+        warm_acc = sums.tile([P, N_TILE], F32, tag="acc")
+
+        def keep_clock_up(times):
+            for turn in range(times):
+                nc.tensor.matmul(
+                    out=warm_acc[:], lhsT=ones[:, 0:P], rhs=ones[:], start=True, stop=True
+                )
+
+        keep_clock_up(WARM_BEFORE_LOADS)
+
+        z_view = z0.rearrange("n (p t) j -> p n (t j)", p=P)
+        z_early = const.tile([P, EARLY * STRIP * BOX], F32)
         nc.sync.dma_start(
-            out=z_sb[:].rearrange("p (n f) -> p n f", n=IMAGES),
-            in_=z0.rearrange("n (p t) j -> p n (t j)", p=P),
+            out=z_early[:].rearrange("p (n f) -> p n f", n=EARLY), in_=z_view[:, 0:EARLY, :]
         )
         anchor_rows = const.tile([P, SPREAD_N], BF16)
         nc.vector.memset(anchor_rows[:], 0.0)
         nc.sync.dma_start(out=anchor_rows[0:P:STRIPS, 0:2], in_=anchors[0])
+        first_pieces = []
+        piece_cols = T_PER_BANK * FIELDS
+        g_first = grad_out[0, 0:LEVEL0_ROWS, :].rearrange("(p t) j -> p (t j)", p=P)
+        for piece in range(STRIP // T_PER_BANK):
+            dy_piece = pieces.tile([P, piece_cols], BF16)
+            nc.sync.dma_start(
+                out=dy_piece[:], in_=g_first[:, piece * piece_cols : (piece + 1) * piece_cols]
+            )
+            first_pieces.append(dy_piece)
+        z_late = const.tile([P, (IMAGES - EARLY) * STRIP * BOX], F32)
         w_sb = const.tile([P, ANCHORS * CHANNELS], BF16)
-        dy_tiles = []
-        for n in range(IMAGES):
+        dy_tiles = [None]
+        for n in range(1, IMAGES):
             dy_sb = grads.tile([P, STRIP * FIELDS], BF16)
             nc.sync.dma_start(
                 out=dy_sb[:], in_=grad_out[n, 0:LEVEL0_ROWS, :].rearrange("(p t) j -> p (t j)", p=P)
             )
             dy_tiles.append(dy_sb)
-            if n == 0:
+            if n == 1:
+                nc.sync.dma_start(
+                    out=z_late[:].rearrange("p (n f) -> p n f", n=IMAGES - EARLY),
+                    in_=z_view[:, EARLY:IMAGES, :],
+                )
                 nc.sync.dma_start(
                     out=w_sb[:].rearrange("p (a c) -> p a c", a=ANCHORS),
                     in_=w0.rearrange("(a p) c -> p a c", a=ANCHORS),
                 )
+
+        def rows_of(n, t):
+            if n == 0:
+                i = t % T_PER_BANK
+                return first_pieces[t // T_PER_BANK][:, i * FIELDS : (i + 1) * FIELDS]
+            return dy_tiles[n][:, t * FIELDS : (t + 1) * FIELDS]
 
         identity = const.tile([P, P], BF16)
         masks.make_identity(nc, identity[:])
@@ -100,11 +136,16 @@ def tile_head_t_v_kernel(
         )
         minus_8_anchor = const.tile([P, 2], F32)
         nc.vector.tensor_scalar_mul(out=minus_8_anchor[:], in0=own_anchor[:, 0:2], scalar1=-8.0)
-        sg = const.tile([P, IMAGES * STRIP * BOX], F32)
-        nc.scalar.activation(out=sg[:], in_=z_sb[:], func=ACT.Sigmoid)
+        keep_clock_up(WARM_AFTER_ANCHORS)
+        sg_early = const.tile([P, EARLY * STRIP * BOX], F32)
+        nc.scalar.activation(out=sg_early[:], in_=z_early[:], func=ACT.Sigmoid)
+        sg_late = const.tile([P, (IMAGES - EARLY) * STRIP * BOX], F32)
 
         def scale_box_fields(n):
-            sg_n = sg[:, n * STRIP * BOX : (n + 1) * STRIP * BOX]
+            if n < EARLY:
+                sg_n = sg_early[:, n * STRIP * BOX : (n + 1) * STRIP * BOX]
+            else:
+                sg_n = sg_late[:, (n - EARLY) * STRIP * BOX : (n - EARLY + 1) * STRIP * BOX]
             minus_slope = factors.tile([P, STRIP * BOX], F32)
             nc.vector.scalar_tensor_tensor(
                 out=minus_slope[:], in0=sg_n, scalar=1.0, in1=sg_n, op0=ALU.subtract, op1=ALU.mult
@@ -125,10 +166,17 @@ def tile_head_t_v_kernel(
                     op0=ALU.mult,
                     op1=ALU.mult,
                 )
-            box = dy_tiles[n][:].rearrange("p (t j) -> p t j", j=FIELDS)[:, :, 0:BOX]
-            nc.vector.tensor_tensor(
-                out=box, in0=box, in1=factor[:].rearrange("p (j t) -> p t j", j=BOX), op=ALU.mult
-            )
+            factor_rows = factor[:].rearrange("p (j t) -> p t j", j=BOX)
+            if n == 0:
+                parts = [
+                    (dy_piece, factor_rows[:, k * T_PER_BANK : (k + 1) * T_PER_BANK, :])
+                    for k, dy_piece in enumerate(first_pieces)
+                ]
+            else:
+                parts = [(dy_tiles[n], factor_rows)]
+            for dy_part, factor_part in parts:
+                box = dy_part[:].rearrange("p (t j) -> p t j", j=FIELDS)[:, :, 0:BOX]
+                nc.vector.tensor_tensor(out=box, in0=box, in1=factor_part, op=ALU.mult)
 
         def quantise_weights():
             w_grouped = const.tile([P, C_TILES * P * ANCHORS], BF16, align_bytes=64)
@@ -152,13 +200,15 @@ def tile_head_t_v_kernel(
                     t = half * HALF_T + bank * T_PER_BANK + i
                     nc.tensor.transpose(
                         dy_t[:].rearrange("p (s i a) -> p i s a", i=T_PER_BANK, a=ANCHORS)[:, i],
-                        dy_tiles[n][:, t * FIELDS : (t + 1) * FIELDS],
+                        rows_of(n, t),
                         anchors_together[:],
                     )
                 nc.scalar.copy(
                     out=dy_grouped[:, bank * width : (bank + 1) * width].bitcast(F32),
                     in_=dy_t[:].bitcast(F32),
                 )
+                if n * HALVES + half < 3:
+                    keep_clock_up(1)
             return dy_grouped
 
         def quantise(dy_grouped):
@@ -198,12 +248,14 @@ def tile_head_t_v_kernel(
                 )
 
         scale_box_fields(0)
-        w_codes, w_scales = quantise_weights()
         steps = IMAGES * HALVES
         grouped_of = {}
         operand_of = {}
         out_of = {}
         for step in range(steps + 3):
+            if step == 2:
+                nc.scalar.activation(out=sg_late[:], in_=z_late[:], func=ACT.Sigmoid)
+                w_codes, w_scales = quantise_weights()
             if step < steps:
                 n, half = divmod(step, HALVES)
                 grouped_of[step] = transpose(n, half)

@@ -59,6 +59,9 @@ def tile_head_t_v_kernel(
         flipped = ctx.enter_context(tc.psum_pool(name="flipped", bufs=4))
         sums = ctx.enter_context(tc.psum_pool(name="sums", bufs=4))
 
+        anchor_rows = const.tile([P, SPREAD_N], BF16)
+        nc.vector.memset(anchor_rows[:], 0.0)
+
         ones = const.tile([P, N_TILE], BF16)
         nc.vector.memset(ones[:], 1.0)
         warm_acc = sums.tile([P, N_TILE], F32, tag="acc")
@@ -76,9 +79,6 @@ def tile_head_t_v_kernel(
         nc.sync.dma_start(
             out=z_early[:].rearrange("p (n f) -> p n f", n=EARLY), in_=z_view[:, 0:EARLY, :]
         )
-        anchor_rows = const.tile([P, SPREAD_N], BF16)
-        nc.vector.memset(anchor_rows[:], 0.0)
-        nc.sync.dma_start(out=anchor_rows[0:P:STRIPS, 0:2], in_=anchors[0])
         first_pieces = []
         piece_cols = T_PER_BANK * FIELDS
         g_first = grad_out[0, 0:LEVEL0_ROWS, :].rearrange("(p t) j -> p (t j)", p=P)
@@ -88,6 +88,8 @@ def tile_head_t_v_kernel(
                 out=dy_piece[:], in_=g_first[:, piece * piece_cols : (piece + 1) * piece_cols]
             )
             first_pieces.append(dy_piece)
+            if piece == 1:
+                nc.sync.dma_start(out=anchor_rows[0:P:STRIPS, 0:2], in_=anchors[0])
         z_late = const.tile([P, (IMAGES - EARLY) * STRIP * BOX], F32)
         w_sb = const.tile([P, ANCHORS * CHANNELS], BF16)
         dy_tiles = [None]

from contextlib import ExitStack

import concourse.masks as masks
import concourse.mybir as mybir

F32 = mybir.dt.float32
BF16 = mybir.dt.bfloat16
U32 = mybir.dt.uint32
U8 = mybir.dt.uint8
E4M3_X4 = mybir.dt.float8_e4m3fn_x4
E5M2_X4 = mybir.dt.float8_e5m2_x4
ALU = mybir.AluOpType
ACT = mybir.ActivationFunctionType

P = 128
IMAGES = 6
ANCHORS = 4
FIELDS = 128
BOX = 4
POSITIONS = 1024
CHANNELS = 512
LEVEL0_ROWS = ANCHORS * POSITIONS

STRIPS = P // ANCHORS
STRIP = POSITIONS // STRIPS
N_TILE = 512
HALF_T = N_TILE // STRIPS
HALVES = STRIP // HALF_T
T_PER_BANK = 8
C_TILES = CHANNELS // P
SPREAD_N = 32
EARLY = 2
WARM_BEFORE_LOADS = 6
WARM_AFTER_ANCHORS = 2
C_TILES_PER_STEP = 2

FLOPS = 2 * ANCHORS * FIELDS * CHANNELS * IMAGES * POSITIONS
BYTES = (
    2 * IMAGES * LEVEL0_ROWS * FIELDS
    + 4 * IMAGES * LEVEL0_ROWS * BOX
    + 2 * ANCHORS * FIELDS * CHANNELS
    + 2 * ANCHORS * 2
    + 4 * IMAGES * CHANNELS * POSITIONS
)


def tile_head_t_v_kernel(
    tc, f0, f1, f2, w0, b0, w1, b1, w2, b2, anchors, z0, grad_out, out
):
    nc = tc.nc
    with ExitStack() as ctx:
        ctx.enter_context(tc.manual_schedule())
        const = ctx.enter_context(tc.tile_pool(name="const", bufs=1))
        pieces = ctx.enter_context(tc.tile_pool(name="pieces", bufs=STRIP // T_PER_BANK))
        grads = ctx.enter_context(tc.tile_pool(name="grads", bufs=IMAGES - 1))
        factors = ctx.enter_context(tc.tile_pool(name="factors", bufs=2))
        operands = ctx.enter_context(tc.tile_pool(name="operands", bufs=6))
        results = ctx.enter_context(tc.tile_pool(name="results", bufs=4))
        flipped = ctx.enter_context(tc.psum_pool(name="flipped", bufs=4))
        sums = ctx.enter_context(tc.psum_pool(name="sums", bufs=4))

        anchor_rows = const.tile([P, SPREAD_N], BF16)
        nc.vector.memset(anchor_rows[:], 0.0)

        ones = const.tile([P, N_TILE], BF16)
        nc.vector.memset(ones[:], 1.0)
        warm_acc = sums.tile([P, N_TILE], F32, tag="acc")

        def keep_clock_up(times):
            for turn in range(times):
                nc.tensor.matmul(
                    out=warm_acc[:], lhsT=ones[:, 0:P], rhs=ones[:], start=True, stop=True
                )

        keep_clock_up(WARM_BEFORE_LOADS)

        z_view = z0.rearrange("n (p t) j -> p n (t j)", p=P)
        z_early = const.tile([P, EARLY * STRIP * BOX], F32)
        nc.sync.dma_start(
            out=z_early[:].rearrange("p (n f) -> p n f", n=EARLY), in_=z_view[:, 0:EARLY, :]
        )
        first_pieces = []
        piece_cols = T_PER_BANK * FIELDS
        g_first = grad_out[0, 0:LEVEL0_ROWS, :].rearrange("(p t) j -> p (t j)", p=P)
        for piece in range(STRIP // T_PER_BANK):
            dy_piece = pieces.tile([P, piece_cols], BF16)
            nc.sync.dma_start(
                out=dy_piece[:], in_=g_first[:, piece * piece_cols : (piece + 1) * piece_cols]
            )
            first_pieces.append(dy_piece)
            if piece == 1:
                nc.sync.dma_start(out=anchor_rows[0:P:STRIPS, 0:2], in_=anchors[0])
        z_late = const.tile([P, (IMAGES - EARLY) * STRIP * BOX], F32)
        w_sb = const.tile([P, ANCHORS * CHANNELS], BF16)
        dy_tiles = [None]
        for n in range(1, IMAGES):
            dy_sb = grads.tile([P, STRIP * FIELDS], BF16)
            nc.sync.dma_start(
                out=dy_sb[:], in_=grad_out[n, 0:LEVEL0_ROWS, :].rearrange("(p t) j -> p (t j)", p=P)
            )
            dy_tiles.append(dy_sb)
            if n == 1:
                nc.sync.dma_start(
                    out=z_late[:].rearrange("p (n f) -> p n f", n=IMAGES - EARLY),
                    in_=z_view[:, EARLY:IMAGES, :],
                )
                nc.sync.dma_start(
                    out=w_sb[:].rearrange("p (a c) -> p a c", a=ANCHORS),
                    in_=w0.rearrange("(a p) c -> p a c", a=ANCHORS),
                )

        def rows_of(n, t):
            if n == 0:
                i = t % T_PER_BANK
                return first_pieces[t // T_PER_BANK][:, i * FIELDS : (i + 1) * FIELDS]
            return dy_tiles[n][:, t * FIELDS : (t + 1) * FIELDS]

        identity = const.tile([P, P], BF16)
        masks.make_identity(nc, identity[:])
        anchors_together = const.tile([P, P], BF16)
        nc.vector.tensor_copy(
            out=anchors_together[:].rearrange("p (s a) -> p s a", a=ANCHORS),
            in_=identity[:].rearrange("p (a s) -> p s a", a=ANCHORS),
        )

        same_anchor = const.tile([P, P], BF16)
        nc.vector.memset(same_anchor[:], 0.0)
        for a in range(ANCHORS):
            block = slice(a * STRIPS, (a + 1) * STRIPS)
            nc.vector.memset(same_anchor[block, block], 1.0)
        own_anchor = sums.tile([P, N_TILE], F32, tag="acc")
        nc.tensor.matmul(
            out=own_anchor[:, 0:SPREAD_N],
            lhsT=same_anchor[:],
            rhs=anchor_rows[:],
            start=True,
            stop=True,
        )
        minus_8_anchor = const.tile([P, 2], F32)
        nc.vector.tensor_scalar_mul(out=minus_8_anchor[:], in0=own_anchor[:, 0:2], scalar1=-8.0)
        keep_clock_up(WARM_AFTER_ANCHORS)
        sg_early = const.tile([P, EARLY * STRIP * BOX], F32)
        nc.scalar.activation(out=sg_early[:], in_=z_early[:], func=ACT.Sigmoid)
        sg_late = const.tile([P, (IMAGES - EARLY) * STRIP * BOX], F32)

        def scale_box_fields(n):
            if n < EARLY:
                sg_n = sg_early[:, n * STRIP * BOX : (n + 1) * STRIP * BOX]
            else:
                sg_n = sg_late[:, (n - EARLY) * STRIP * BOX : (n - EARLY + 1) * STRIP * BOX]
            minus_slope = factors.tile([P, STRIP * BOX], F32)
            nc.vector.scalar_tensor_tensor(
                out=minus_slope[:], in0=sg_n, scalar=1.0, in1=sg_n, op0=ALU.subtract, op1=ALU.mult
            )
            factor = factors.tile([P, BOX * STRIP], F32)
            factor_planes = factor[:].rearrange("p (j t) -> p j t", j=BOX)
            sg_planes = sg_n.rearrange("p (t j) -> p j t", j=BOX)
            minus_slope_planes = minus_slope[:].rearrange("p (t j) -> p j t", j=BOX)
            nc.vector.tensor_scalar_mul(
                out=factor_planes[:, 0:2, :], in0=minus_slope_planes[:, 0:2, :], scalar1=-2.0
            )
            for c in range(2):
                nc.vector.scalar_tensor_tensor(
                    out=factor_planes[:, 2 + c, :],
                    in0=minus_slope_planes[:, 2 + c, :],
                    scalar=minus_8_anchor[:, c : c + 1],
                    in1=sg_planes[:, 2 + c, :],
                    op0=ALU.mult,
                    op1=ALU.mult,
                )
            factor_rows = factor[:].rearrange("p (j t) -> p t j", j=BOX)
            if n == 0:
                parts = [
                    (dy_piece, factor_rows[:, k * T_PER_BANK : (k + 1) * T_PER_BANK, :])
                    for k, dy_piece in enumerate(first_pieces)
                ]
            else:
                parts = [(dy_tiles[n], factor_rows)]
            for dy_part, factor_part in parts:
                box = dy_part[:].rearrange("p (t j) -> p t j", j=FIELDS)[:, :, 0:BOX]
                nc.vector.tensor_tensor(out=box, in0=box, in1=factor_part, op=ALU.mult)

        def quantise_weights():
            w_grouped = const.tile([P, C_TILES * P * ANCHORS], BF16, align_bytes=64)
            nc.vector.tensor_copy(
                out=w_grouped[:].rearrange("p (ct m a) -> p ct m a", ct=C_TILES, a=ANCHORS),
                in_=w_sb[:].rearrange("p (a m ct) -> p ct m a", a=ANCHORS, ct=C_TILES),
            )
            w_codes = const.tile([P, CHANNELS], U32, align_bytes=64)
            w_scales = const.tile([P, CHANNELS], U8, align_bytes=64)
            nc.vector.quantize_mx(
                out=w_codes[:].bitcast(E4M3_X4), scales=w_scales[:], in_=w_grouped[:]
            )
            return w_codes, w_scales

        def transpose(n, half):
            dy_grouped = operands.tile([P, N_TILE * ANCHORS], BF16, align_bytes=64)
            width = T_PER_BANK * P
            for bank in range(HALF_T // T_PER_BANK):
                dy_t = flipped.tile([P, width], BF16)
                for i in range(T_PER_BANK):
                    t = half * HALF_T + bank * T_PER_BANK + i
                    nc.tensor.transpose(
                        dy_t[:].rearrange("p (s i a) -> p i s a", i=T_PER_BANK, a=ANCHORS)[:, i],
                        rows_of(n, t),
                        anchors_together[:],
                    )
                nc.scalar.copy(
                    out=dy_grouped[:, bank * width : (bank + 1) * width].bitcast(F32),
                    in_=dy_t[:].bitcast(F32),
                )
                if n * HALVES + half < 3:
                    keep_clock_up(1)
            return dy_grouped

        def quantise(dy_grouped):
            dy_codes = operands.tile([P, N_TILE], U32, align_bytes=64)
            dy_scales = operands.tile([P, N_TILE], U8, align_bytes=64)
            nc.vector.quantize_mx(
                out=dy_codes[:].bitcast(E5M2_X4), scales=dy_scales[:], in_=dy_grouped[:]
            )
            return dy_codes, dy_scales

        def multiply(n, pair, operand_of_half, out_sb):
            out_view = out_sb[:].rearrange(
                "p (ct s h b i) -> p ct h b s i", ct=C_TILES, s=STRIPS, h=HALVES, i=T_PER_BANK
            )
            for ct in range(pair * C_TILES_PER_STEP, (pair + 1) * C_TILES_PER_STEP):
                for half in range(HALVES):
                    dy_codes, dy_scales = operand_of_half[half]
                    acc = sums.tile([P, N_TILE], F32)
                    nc.tensor.matmul_mx(
                        out=acc[:],
                        lhsT=w_codes[:, ct * P : (ct + 1) * P].bitcast(E4M3_X4),
                        lhsT_scale=w_scales[:, ct * P : (ct + 1) * P],
                        rhs=dy_codes[:].bitcast(E5M2_X4),
                        rhs_scale=dy_scales[:],
                        start=True,
                        stop=True,
                    )
                    copy_out = nc.scalar.copy if half == 0 else nc.vector.tensor_copy
                    copy_out(
                        out=out_view[:, ct, half],
                        in_=acc[:].rearrange("p (b s i) -> p b s i", s=STRIPS, i=T_PER_BANK),
                    )
                cols = slice(ct * POSITIONS, (ct + 1) * POSITIONS)
                nc.sync.dma_start(
                    out=out[n].rearrange("(m ct) u v -> m (ct u v)", ct=C_TILES)[:, cols],
                    in_=out_sb[:, cols],
                )

        scale_box_fields(0)
        steps = IMAGES * HALVES
        grouped_of = {}
        operand_of = {}
        out_of = {}
        for step in range(steps + 3):
            if step == 2:
                nc.scalar.activation(out=sg_late[:], in_=z_late[:], func=ACT.Sigmoid)
                w_codes, w_scales = quantise_weights()
            if step < steps:
                n, half = divmod(step, HALVES)
                grouped_of[step] = transpose(n, half)
            if 1 <= step <= steps:
                operand_of[step - 1] = quantise(grouped_of[step - 1])
            if step >= 3:
                n, pair = divmod(step - 3, C_TILES // C_TILES_PER_STEP)
                if pair == 0:
                    out_sb = results.tile([P, C_TILES * POSITIONS], F32)
                    out_of[n] = out_sb
                multiply(n, pair, [operand_of[n * HALVES + h] for h in range(HALVES)], out_of[n])
            if step < steps and step % HALVES == 0 and step // HALVES + 1 < IMAGES:
                scale_box_fields(step // HALVES + 1)
